import numpy as np
import ml_dtypes


def mxq(x, axis, fmt="e4m3"):
    dtype, down = {"e4m3": (ml_dtypes.float8_e4m3fn, 7), "e5m2": (ml_dtypes.float8_e5m2, 14)}[fmt]
    v = np.moveaxis(np.asarray(x, np.float32).astype(ml_dtypes.bfloat16).astype(np.float64), axis, -1)
    blocks = v.reshape(v.shape[:-1] + (-1, 32))
    amax = np.abs(blocks).max(-1, keepdims=True)
    byte = np.maximum(np.where(amax > 0, np.frexp(amax)[1] - 1 + 127, 0) - down, 1)
    scale = np.exp2(byte - 127.0)
    codes = (blocks / scale).astype(np.float32).astype(dtype).astype(np.float64)
    return np.moveaxis((codes * scale).reshape(v.shape), -1, axis)


WIDE = False


def mx_kscale(k):
    if not WIDE:
        return np.ones(k)
    levels = np.array([10, -10, 5, -5, 0])
    a = np.random.permutation(np.resize(levels, k // 512 * 4)).reshape(k // 512, 4)
    idx = np.arange(k)
    return np.exp2(a[idx // 512, idx % 128 // 32])


BF16 = ml_dtypes.bfloat16


def bf(x):
    return np.asarray(x, np.float32).astype(BF16)


def f64(x):
    return np.asarray(x).astype(np.float64)


B, S, D, DFF, R = 4, 160, 256, 16384, 512


def setup_inputs():
    t, r = mx_kscale(DFF), mx_kscale(R)
    v = np.random.standard_normal((B, S, DFF)) * 1.2
    return {"h_gelu": bf(v / (1.0 + np.exp(-1.702 * v)) * t),
            "c_proj_U": bf(np.random.standard_normal((DFF, R)) * 2.0 / np.sqrt(DFF) / t[:, None]),
            "c_proj_S": bf(np.random.uniform(size=R) * r),
            "c_proj_V": bf(np.random.standard_normal((D, R)) / np.sqrt(R) / r[None, :]),
            "c_proj_bias": bf(np.random.standard_normal(D) * 0.3)}


def reference(h_gelu, c_proj_U, c_proj_S, c_proj_V, c_proj_bias):
    us = f64(c_proj_U) * f64(c_proj_S)[None, :]
    w = mxq(us, 1, "e4m3") @ mxq(f64(c_proj_V), 1, "e4m3").T
    return (mxq(f64(h_gelu), 2, "e4m3") @ mxq(w, 0, "e4m3")) + f64(c_proj_bias)

@@ -1,0 +1,261 @@
+from contextlib import ExitStack
+
+import concourse.mybir as mybir
+from concourse.masks import make_identity
+
+BF16 = mybir.dt.bfloat16
+F32 = mybir.dt.float32
+U32 = mybir.dt.uint32
+U8 = mybir.dt.uint8
+FP8X4 = mybir.dt.float8_e4m3fn_x4
+
+P = 128
+PACK = 4
+K_PASS = P * PACK
+
+TOKENS = 640
+TOKEN_BLOCKS = TOKENS // P
+DFF = 16384
+RANK = 512
+D = 256
+D_HALVES = D // P
+
+PASSES_PER_ROUND = 2
+ROUND_K = PASSES_PER_ROUND * K_PASS
+ROUNDS = DFF // ROUND_K
+BANK_F32 = 512
+BANK_COLS = BANK_F32 // 2
+U_BANKS = ROUND_K // BANK_COLS
+H_COLS = PASSES_PER_ROUND * TOKENS
+H_BANKS = H_COLS // BANK_COLS
+QUANT_MAX_COLS = 1024
+
+LOADS_AHEAD = 5
+RING_BANKS = 8 - TOKEN_BLOCKS
+
+FLOPS = 2 * DFF * RANK * D + 2 * TOKENS * DFF * D
+
+
+def tile_hybridsuperlayer_pb_k_kernel(
+    tc, h_gelu, c_proj_U, c_proj_S, c_proj_V, c_proj_bias, out
+):
+    nc = tc.nc
+    mult = mybir.AluOpType.mult
+    add = mybir.AluOpType.add
+
+    h_view = h_gelu.flatten_outer_dims().rearrange("(b p) (i k) -> i p b k", p=P, k=ROUND_K)
+    u_view = c_proj_U.rearrange("(i x p e) r -> i p x (e r)", x=2 * PASSES_PER_ROUND, p=P, e=2)
+    out_view = out.flatten_outer_dims().rearrange("(b p) d -> b p d", p=P)
+
+    with ExitStack() as ctx:
+        consts = ctx.enter_context(tc.tile_pool(name="consts", bufs=1))
+        loads = ctx.enter_context(tc.tile_pool(name="loads", bufs=LOADS_AHEAD))
+        work = ctx.enter_context(tc.tile_pool(name="work", bufs=2))
+        acc_pool = ctx.enter_context(tc.psum_pool(name="acc", bufs=1))
+        ring = ctx.enter_context(tc.psum_pool(name="ring", bufs=RING_BANKS))
+        ctx.enter_context(tc.manual_schedule())
+
+        u_rows = {}
+        h_rows = {}
+
+        def load(i):
+            u_rows[i] = loads.tile([P, 2 * PASSES_PER_ROUND, 2 * RANK], BF16, name="u_rows")
+            nc.sync.dma_start(out=u_rows[i][:], in_=u_view[i])
+            h_rows[i] = loads.tile([P, TOKEN_BLOCKS, ROUND_K], BF16, name="h_rows")
+            nc.sync.dma_start(out=h_rows[i][:], in_=h_view[i])
+
+        def empty_bank(dest, bank_view, on_vector):
+            if on_vector:
+                nc.vector.tensor_copy(out=dest, in_=bank_view)
+            else:
+                nc.scalar.copy(out=dest, in_=bank_view)
+
+        v_rows = consts.tile([P, D_HALVES, RANK], BF16)
+        nc.scalar.dma_start(out=v_rows[:], in_=c_proj_V.rearrange("(x p) r -> p x r", p=P))
+        s_word = consts.tile([P, 2, 2], BF16)
+        with nc.allow_non_contiguous_dma(reason="512 values, two pairs to a partition, once"):
+            nc.scalar.dma_start(
+                out=s_word[:], in_=c_proj_S.rearrange("(half p e) -> p half e", half=2, p=P, e=2)
+            )
+        bias_all = consts.tile([P, D], BF16)
+        nc.scalar.dma_start(out=bias_all[:], in_=c_proj_bias.partition_broadcast(P))
+        for i in range(LOADS_AHEAD):
+            load(i)
+
+        ident = consts.tile([P, P], F32)
+        make_identity(nc, ident[:])
+
+        s_pass = consts.tile([P, K_PASS, PACK], BF16)
+        nc.vector.tensor_copy(
+            out=s_pass[:],
+            in_=s_word[:].rearrange("p half e -> p (half e)").unsqueeze(1).to_broadcast([P, K_PASS, PACK]),
+        )
+
+        v_words = v_rows[:].bitcast(F32)
+        v_bank = ring.tile([P, 2, BANK_COLS], F32, tag="bank")
+        for x in range(D_HALVES):
+            for half in range(2):
+                nc.tensor.transpose(
+                    v_bank[:, half, x * P : (x + 1) * P],
+                    v_words[:, x, half * P : (half + 1) * P],
+                    ident[:],
+                )
+        v_t = consts.tile([P, D, PACK], BF16, align_bytes=64)
+        empty_bank(v_t[:].bitcast(F32), v_bank[:].rearrange("p half c -> p c half"), False)
+        v_codes = consts.tile([P, D], U32, align_bytes=64)
+        v_scales = consts.tile([P, D], U8, align_bytes=64)
+        nc.vector.quantize_mx(
+            out=v_codes[:].bitcast(FP8X4),
+            scales=v_scales[:],
+            in_=v_t[:].rearrange("p c t -> p (c t)"),
+        )
+
+        acc = [acc_pool.tile([P, D], F32, name="acc%d" % b) for b in range(TOKEN_BLOCKS)]
+
+        u_t = {}
+        us_t = {}
+        us_codes = {}
+        us_scales = {}
+        h_t = {}
+        h_codes = {}
+        h_scales = {}
+        w_t = {}
+        w_codes = {}
+        w_scales = {}
+
+        def transpose_u(i):
+            u_words = u_rows[i][:].bitcast(F32)
+            u_t[i] = work.tile([P, ROUND_K, PACK], BF16, name="u_t", align_bytes=64)
+            u_t_words = u_t[i][:].bitcast(F32)
+            for x in range(U_BANKS):
+                bank = ring.tile([P, 2, BANK_COLS], F32, tag="bank", name="u_bank")
+                for e in range(2):
+                    for half in range(2):
+                        nc.tensor.transpose(
+                            bank[:, half, e * P : (e + 1) * P],
+                            u_words[:, x, e * (RANK // 2) + half * P : e * (RANK // 2) + (half + 1) * P],
+                            ident[:],
+                        )
+                empty_bank(
+                    u_t_words[:, x * BANK_COLS : (x + 1) * BANK_COLS, :],
+                    bank[:].rearrange("p half c -> p c half"),
+                    False,
+                )
+
+        def scale_u(i):
+            us_t[i] = work.tile([P, ROUND_K, PACK], BF16, name="us_t", align_bytes=64)
+            for g in range(PASSES_PER_ROUND):
+                cols = slice(g * K_PASS, (g + 1) * K_PASS)
+                nc.vector.tensor_tensor(
+                    out=us_t[i][:, cols, :], in0=u_t[i][:, cols, :], in1=s_pass[:], op=mult
+                )
+
+        def quantise_us(i):
+            us_codes[i] = work.tile([P, ROUND_K], U32, name="us_codes", align_bytes=64)
+            us_scales[i] = work.tile([P, ROUND_K], U8, name="us_scales", align_bytes=64)
+            nc.vector.quantize_mx(
+                out=us_codes[i][:].bitcast(FP8X4),
+                scales=us_scales[i][:],
+                in_=us_t[i][:].rearrange("p c t -> p (c t)"),
+            )
+
+        def transpose_h(i):
+            h_words = h_rows[i][:].bitcast(F32)
+            h_t[i] = work.tile([P, H_COLS, PACK], BF16, name="h_t", align_bytes=64)
+            h_t_words = h_t[i][:].bitcast(F32)
+            for j in range(H_BANKS):
+                bank = ring.tile([P, 2, BANK_COLS], F32, tag="bank", name="h_bank")
+                for y in range(2):
+                    g, b = divmod(2 * j + y, TOKEN_BLOCKS)
+                    for half in range(2):
+                        first = (2 * g + half) * P
+                        nc.tensor.transpose(
+                            bank[:, half, y * P : (y + 1) * P],
+                            h_words[:, b, first : first + P],
+                            ident[:],
+                        )
+                empty_bank(
+                    h_t_words[:, j * BANK_COLS : (j + 1) * BANK_COLS, :],
+                    bank[:].rearrange("p half c -> p c half"),
+                    j == H_BANKS - 1,
+                )
+
+        def quantise_h(i):
+            h_codes[i] = work.tile([P, H_COLS], U32, name="h_codes", bufs=3, align_bytes=64)
+            h_scales[i] = work.tile([P, H_COLS], U8, name="h_scales", bufs=3, align_bytes=64)
+            for first in range(0, H_COLS, QUANT_MAX_COLS):
+                cols = slice(first, min(first + QUANT_MAX_COLS, H_COLS))
+                nc.vector.quantize_mx(
+                    out=h_codes[i][:, cols].bitcast(FP8X4),
+                    scales=h_scales[i][:, cols],
+                    in_=h_t[i][:, cols, :].rearrange("p c t -> p (c t)"),
+                )
+
+        def build_w(i):
+            w_t[i] = work.tile([P, PASSES_PER_ROUND, D, PACK], BF16, name="w_t", align_bytes=64)
+            for g in range(PASSES_PER_ROUND):
+                for x in range(D_HALVES):
+                    d_cols = slice(x * P, (x + 1) * P)
+                    bank = ring.tile([P, PACK, P], F32, tag="bank", name="w_bank")
+                    for t in range(PACK):
+                        k_cols = slice(g * K_PASS + t * P, g * K_PASS + (t + 1) * P)
+                        nc.tensor.matmul_mx(
+                            out=bank[:, t, :],
+                            lhsT=us_codes[i][:, k_cols].bitcast(FP8X4),
+                            lhsT_scale=us_scales[i][:, k_cols],
+                            rhs=v_codes[:, d_cols].bitcast(FP8X4),
+                            rhs_scale=v_scales[:, d_cols],
+                            start=True,
+                            stop=True,
+                        )
+                    empty_bank(
+                        w_t[i][:, g, d_cols, :],
+                        bank[:].rearrange("p t d -> p d t"),
+                        g == PASSES_PER_ROUND - 1 and x == D_HALVES - 1,
+                    )
+
+        def quantise_w(i):
+            w_codes[i] = work.tile([P, PASSES_PER_ROUND * D], U32, name="w_codes", align_bytes=64)
+            w_scales[i] = work.tile([P, PASSES_PER_ROUND * D], U8, name="w_scales", align_bytes=64)
+            nc.vector.quantize_mx(
+                out=w_codes[i][:].bitcast(FP8X4),
+                scales=w_scales[i][:],
+                in_=w_t[i][:].rearrange("p g d t -> p (g d t)"),
+            )
+
+        def apply_w(i):
+            for b in range(TOKEN_BLOCKS):
+                for g in range(PASSES_PER_ROUND):
+                    tok_cols = slice((g * TOKEN_BLOCKS + b) * P, (g * TOKEN_BLOCKS + b + 1) * P)
+                    d_cols = slice(g * D, (g + 1) * D)
+                    nc.tensor.matmul_mx(
+                        out=acc[b][:],
+                        lhsT=h_codes[i][:, tok_cols].bitcast(FP8X4),
+                        lhsT_scale=h_scales[i][:, tok_cols],
+                        rhs=w_codes[i][:, d_cols].bitcast(FP8X4),
+                        rhs_scale=w_scales[i][:, d_cols],
+                        start=(i == 0 and g == 0),
+                        stop=(i == ROUNDS - 1 and g == PASSES_PER_ROUND - 1),
+                    )
+
+        for s in range(ROUNDS + 2):
+            if 1 <= s <= ROUNDS:
+                quantise_h(s - 1)
+            if 2 <= s:
+                quantise_w(s - 2)
+            if s < ROUNDS:
+                transpose_u(s)
+                scale_u(s)
+                transpose_h(s)
+                quantise_us(s)
+                if s + LOADS_AHEAD < ROUNDS:
+                    load(s + LOADS_AHEAD)
+            if 1 <= s <= ROUNDS:
+                build_w(s - 1)
+            if 2 <= s:
+                apply_w(s - 2)
+
+        result = consts.tile([P, TOKEN_BLOCKS, D], F32)
+        for b in range(TOKEN_BLOCKS):
+            nc.vector.tensor_tensor(out=result[:, b, :], in0=acc[b][:], in1=bias_all[:], op=add)
+            nc.sync.dma_start(out=out_view[b], in_=result[:, b, :])

@@ -19,19 +19,19 @@ DFF = 16384
 RANK = 512
 D = 256
 D_HALVES = D // P
+PASSES = DFF // K_PASS
 
-PASSES_PER_ROUND = 2
-ROUND_K = PASSES_PER_ROUND * K_PASS
-ROUNDS = DFF // ROUND_K
 BANK_F32 = 512
 BANK_COLS = BANK_F32 // 2
-U_BANKS = ROUND_K // BANK_COLS
-H_COLS = PASSES_PER_ROUND * TOKENS
-H_BANKS = H_COLS // BANK_COLS
-QUANT_MAX_COLS = 1024
+MOVING_TOKENS = BANK_F32
+MOVING_BLOCKS = MOVING_TOKENS // P
+ACC_BANKS = D_HALVES + 1
+RING_BANKS = 8 - ACC_BANKS
 
-LOADS_AHEAD = 5
-RING_BANKS = 8 - TOKEN_BLOCKS
+PASSES_PER_LOAD = 2
+LOADS = PASSES // PASSES_PER_LOAD
+LOADS_AHEAD = 6
+LOAD_K = PASSES_PER_LOAD * K_PASS
 
 FLOPS = 2 * DFF * RANK * D + 2 * TOKENS * DFF * D
 
@@ -43,14 +43,14 @@ def tile_hybridsuperlayer_pb_k_kernel(
     mult = mybir.AluOpType.mult
     add = mybir.AluOpType.add
 
-    h_view = h_gelu.flatten_outer_dims().rearrange("(b p) (i k) -> i p b k", p=P, k=ROUND_K)
-    u_view = c_proj_U.rearrange("(i x p e) r -> i p x (e r)", x=2 * PASSES_PER_ROUND, p=P, e=2)
-    out_view = out.flatten_outer_dims().rearrange("(b p) d -> b p d", p=P)
+    h_view = h_gelu.flatten_outer_dims().rearrange("(b p) (i k) -> i p b k", p=P, k=LOAD_K)
+    u_view = c_proj_U.rearrange("(i x p e) r -> i p x (e r)", x=2 * PASSES_PER_LOAD, p=P, e=2)
+    out_view = out.flatten_outer_dims().rearrange("(b p) d -> p b d", p=P)
 
     with ExitStack() as ctx:
         consts = ctx.enter_context(tc.tile_pool(name="consts", bufs=1))
         loads = ctx.enter_context(tc.tile_pool(name="loads", bufs=LOADS_AHEAD))
-        work = ctx.enter_context(tc.tile_pool(name="work", bufs=2))
+        work = ctx.enter_context(tc.tile_pool(name="work", bufs=3))
         acc_pool = ctx.enter_context(tc.psum_pool(name="acc", bufs=1))
         ring = ctx.enter_context(tc.psum_pool(name="ring", bufs=RING_BANKS))
         ctx.enter_context(tc.manual_schedule())
@@ -59,16 +59,10 @@ def tile_hybridsuperlayer_pb_k_kernel(
         h_rows = {}
 
         def load(i):
-            u_rows[i] = loads.tile([P, 2 * PASSES_PER_ROUND, 2 * RANK], BF16, name="u_rows")
+            u_rows[i] = loads.tile([P, 2 * PASSES_PER_LOAD, 2 * RANK], BF16, name="u_rows")
             nc.sync.dma_start(out=u_rows[i][:], in_=u_view[i])
-            h_rows[i] = loads.tile([P, TOKEN_BLOCKS, ROUND_K], BF16, name="h_rows")
+            h_rows[i] = loads.tile([P, TOKEN_BLOCKS, LOAD_K], BF16, name="h_rows")
             nc.sync.dma_start(out=h_rows[i][:], in_=h_view[i])
-
-        def empty_bank(dest, bank_view, on_vector):
-            if on_vector:
-                nc.vector.tensor_copy(out=dest, in_=bank_view)
-            else:
-                nc.scalar.copy(out=dest, in_=bank_view)
 
         v_rows = consts.tile([P, D_HALVES, RANK], BF16)
         nc.scalar.dma_start(out=v_rows[:], in_=c_proj_V.rearrange("(x p) r -> p x r", p=P))
@@ -101,7 +95,7 @@ def tile_hybridsuperlayer_pb_k_kernel(
                     ident[:],
                 )
         v_t = consts.tile([P, D, PACK], BF16, align_bytes=64)
-        empty_bank(v_t[:].bitcast(F32), v_bank[:].rearrange("p half c -> p c half"), False)
+        nc.scalar.copy(out=v_t[:].bitcast(F32), in_=v_bank[:].rearrange("p half c -> p c half"))
         v_codes = consts.tile([P, D], U32, align_bytes=64)
         v_scales = consts.tile([P, D], U8, align_bytes=64)
         nc.vector.quantize_mx(
@@ -110,7 +104,8 @@ def tile_hybridsuperlayer_pb_k_kernel(
             in_=v_t[:].rearrange("p c t -> p (c t)"),
         )
 
-        acc = [acc_pool.tile([P, D], F32, name="acc%d" % b) for b in range(TOKEN_BLOCKS)]
+        acc_t = [acc_pool.tile([P, MOVING_TOKENS], F32, name="acc_t%d" % x) for x in range(D_HALVES)]
+        acc_last = acc_pool.tile([P, D], F32)
 
         u_t = {}
         us_t = {}
@@ -123,139 +118,166 @@ def tile_hybridsuperlayer_pb_k_kernel(
         w_codes = {}
         w_scales = {}
 
-        def transpose_u(i):
+        def transpose_u(g):
+            i, g_in_load = divmod(g, PASSES_PER_LOAD)
             u_words = u_rows[i][:].bitcast(F32)
-            u_t[i] = work.tile([P, ROUND_K, PACK], BF16, name="u_t", align_bytes=64)
-            u_t_words = u_t[i][:].bitcast(F32)
-            for x in range(U_BANKS):
+            u_t[g] = work.tile([P, K_PASS, PACK], BF16, name="u_t", align_bytes=64)
+            u_t_words = u_t[g][:].bitcast(F32)
+            for k_half in range(2):
                 bank = ring.tile([P, 2, BANK_COLS], F32, tag="bank", name="u_bank")
                 for e in range(2):
                     for half in range(2):
+                        first = e * (RANK // 2) + half * P
                         nc.tensor.transpose(
                             bank[:, half, e * P : (e + 1) * P],
-                            u_words[:, x, e * (RANK // 2) + half * P : e * (RANK // 2) + (half + 1) * P],
+                            u_words[:, 2 * g_in_load + k_half, first : first + P],
                             ident[:],
                         )
-                empty_bank(
-                    u_t_words[:, x * BANK_COLS : (x + 1) * BANK_COLS, :],
-                    bank[:].rearrange("p half c -> p c half"),
-                    False,
+                nc.scalar.copy(
+                    out=u_t_words[:, k_half * BANK_COLS : (k_half + 1) * BANK_COLS, :],
+                    in_=bank[:].rearrange("p half c -> p c half"),
                 )
 
-        def scale_u(i):
-            us_t[i] = work.tile([P, ROUND_K, PACK], BF16, name="us_t", align_bytes=64)
-            for g in range(PASSES_PER_ROUND):
-                cols = slice(g * K_PASS, (g + 1) * K_PASS)
-                nc.vector.tensor_tensor(
-                    out=us_t[i][:, cols, :], in0=u_t[i][:, cols, :], in1=s_pass[:], op=mult
-                )
+        def scale_u(g):
+            us_t[g] = work.tile([P, K_PASS, PACK], BF16, name="us_t", align_bytes=64)
+            nc.vector.tensor_tensor(out=us_t[g][:], in0=u_t[g][:], in1=s_pass[:], op=mult)
 
-        def quantise_us(i):
-            us_codes[i] = work.tile([P, ROUND_K], U32, name="us_codes", align_bytes=64)
-            us_scales[i] = work.tile([P, ROUND_K], U8, name="us_scales", align_bytes=64)
+        def quantise_us(g):
+            us_codes[g] = work.tile([P, K_PASS], U32, name="us_codes", align_bytes=64)
+            us_scales[g] = work.tile([P, K_PASS], U8, name="us_scales", align_bytes=64)
             nc.vector.quantize_mx(
-                out=us_codes[i][:].bitcast(FP8X4),
-                scales=us_scales[i][:],
-                in_=us_t[i][:].rearrange("p c t -> p (c t)"),
+                out=us_codes[g][:].bitcast(FP8X4),
+                scales=us_scales[g][:],
+                in_=us_t[g][:].rearrange("p c t -> p (c t)"),
             )
 
-        def transpose_h(i):
+        def transpose_h(g):
+            i, g_in_load = divmod(g, PASSES_PER_LOAD)
             h_words = h_rows[i][:].bitcast(F32)
-            h_t[i] = work.tile([P, H_COLS, PACK], BF16, name="h_t", align_bytes=64)
-            h_t_words = h_t[i][:].bitcast(F32)
-            for j in range(H_BANKS):
+            h_t[g] = work.tile([P, TOKENS, PACK], BF16, name="h_t", align_bytes=64)
+            h_t_words = h_t[g][:].bitcast(F32)
+            for first_col in range(0, TOKENS, BANK_COLS):
+                cols = min(BANK_COLS, TOKENS - first_col)
                 bank = ring.tile([P, 2, BANK_COLS], F32, tag="bank", name="h_bank")
-                for y in range(2):
-                    g, b = divmod(2 * j + y, TOKEN_BLOCKS)
+                for y in range(cols // P):
                     for half in range(2):
-                        first = (2 * g + half) * P
+                        first = (2 * g_in_load + half) * P
                         nc.tensor.transpose(
                             bank[:, half, y * P : (y + 1) * P],
-                            h_words[:, b, first : first + P],
+                            h_words[:, first_col // P + y, first : first + P],
                             ident[:],
                         )
-                empty_bank(
-                    h_t_words[:, j * BANK_COLS : (j + 1) * BANK_COLS, :],
-                    bank[:].rearrange("p half c -> p c half"),
-                    j == H_BANKS - 1,
-                )
+                dest = h_t_words[:, first_col : first_col + cols, :]
+                filled = bank[:, :, 0:cols].rearrange("p half c -> p c half")
+                if cols == BANK_COLS:
+                    nc.scalar.copy(out=dest, in_=filled)
+                else:
+                    nc.vector.tensor_copy(out=dest, in_=filled)
 
-        def quantise_h(i):
-            h_codes[i] = work.tile([P, H_COLS], U32, name="h_codes", bufs=3, align_bytes=64)
-            h_scales[i] = work.tile([P, H_COLS], U8, name="h_scales", bufs=3, align_bytes=64)
-            for first in range(0, H_COLS, QUANT_MAX_COLS):
-                cols = slice(first, min(first + QUANT_MAX_COLS, H_COLS))
+        def quantise_h(g):
+            h_codes[g] = work.tile([P, TOKENS], U32, name="h_codes", align_bytes=64)
+            h_scales[g] = work.tile([P, TOKENS], U8, name="h_scales", align_bytes=64)
+            for cols in (slice(0, MOVING_TOKENS), slice(MOVING_TOKENS, TOKENS)):
                 nc.vector.quantize_mx(
-                    out=h_codes[i][:, cols].bitcast(FP8X4),
-                    scales=h_scales[i][:, cols],
-                    in_=h_t[i][:, cols, :].rearrange("p c t -> p (c t)"),
+                    out=h_codes[g][:, cols].bitcast(FP8X4),
+                    scales=h_scales[g][:, cols],
+                    in_=h_t[g][:, cols, :].rearrange("p c t -> p (c t)"),
                 )
 
-        def build_w(i):
-            w_t[i] = work.tile([P, PASSES_PER_ROUND, D, PACK], BF16, name="w_t", align_bytes=64)
-            for g in range(PASSES_PER_ROUND):
-                for x in range(D_HALVES):
-                    d_cols = slice(x * P, (x + 1) * P)
-                    bank = ring.tile([P, PACK, P], F32, tag="bank", name="w_bank")
-                    for t in range(PACK):
-                        k_cols = slice(g * K_PASS + t * P, g * K_PASS + (t + 1) * P)
-                        nc.tensor.matmul_mx(
-                            out=bank[:, t, :],
-                            lhsT=us_codes[i][:, k_cols].bitcast(FP8X4),
-                            lhsT_scale=us_scales[i][:, k_cols],
-                            rhs=v_codes[:, d_cols].bitcast(FP8X4),
-                            rhs_scale=v_scales[:, d_cols],
-                            start=True,
-                            stop=True,
-                        )
-                    empty_bank(
-                        w_t[i][:, g, d_cols, :],
-                        bank[:].rearrange("p t d -> p d t"),
-                        g == PASSES_PER_ROUND - 1 and x == D_HALVES - 1,
+        def build_w(g):
+            w_t[g] = work.tile([P, D, PACK], BF16, name="w_t", align_bytes=64)
+            for x in range(D_HALVES):
+                d_cols = slice(x * P, (x + 1) * P)
+                bank = ring.tile([P, PACK, P], F32, tag="bank", name="w_bank")
+                for t in range(PACK):
+                    k_cols = slice(t * P, (t + 1) * P)
+                    nc.tensor.matmul_mx(
+                        out=bank[:, t, :],
+                        lhsT=us_codes[g][:, k_cols].bitcast(FP8X4),
+                        lhsT_scale=us_scales[g][:, k_cols],
+                        rhs=v_codes[:, d_cols].bitcast(FP8X4),
+                        rhs_scale=v_scales[:, d_cols],
+                        start=True,
+                        stop=True,
                     )
+                nc.scalar.copy(out=w_t[g][:, d_cols, :], in_=bank[:].rearrange("p t d -> p d t"))
 
-        def quantise_w(i):
-            w_codes[i] = work.tile([P, PASSES_PER_ROUND * D], U32, name="w_codes", align_bytes=64)
-            w_scales[i] = work.tile([P, PASSES_PER_ROUND * D], U8, name="w_scales", align_bytes=64)
+        def quantise_w(g):
+            w_codes[g] = work.tile([P, D], U32, name="w_codes", align_bytes=64)
+            w_scales[g] = work.tile([P, D], U8, name="w_scales", align_bytes=64)
             nc.vector.quantize_mx(
-                out=w_codes[i][:].bitcast(FP8X4),
-                scales=w_scales[i][:],
-                in_=w_t[i][:].rearrange("p g d t -> p (g d t)"),
+                out=w_codes[g][:].bitcast(FP8X4),
+                scales=w_scales[g][:],
+                in_=w_t[g][:].rearrange("p d t -> p (d t)"),
             )
 
-        def apply_w(i):
-            for b in range(TOKEN_BLOCKS):
-                for g in range(PASSES_PER_ROUND):
-                    tok_cols = slice((g * TOKEN_BLOCKS + b) * P, (g * TOKEN_BLOCKS + b + 1) * P)
-                    d_cols = slice(g * D, (g + 1) * D)
-                    nc.tensor.matmul_mx(
-                        out=acc[b][:],
-                        lhsT=h_codes[i][:, tok_cols].bitcast(FP8X4),
-                        lhsT_scale=h_scales[i][:, tok_cols],
-                        rhs=w_codes[i][:, d_cols].bitcast(FP8X4),
-                        rhs_scale=w_scales[i][:, d_cols],
-                        start=(i == 0 and g == 0),
-                        stop=(i == ROUNDS - 1 and g == PASSES_PER_ROUND - 1),
-                    )
+        def apply_w(g):
+            first_pass = g == 0
+            last_pass = g == PASSES - 1
+            moving = slice(0, MOVING_TOKENS)
+            last_block = slice(MOVING_TOKENS, TOKENS)
+            for x in range(D_HALVES):
+                d_cols = slice(x * P, (x + 1) * P)
+                nc.tensor.matmul_mx(
+                    out=acc_t[x][:],
+                    lhsT=w_codes[g][:, d_cols].bitcast(FP8X4),
+                    lhsT_scale=w_scales[g][:, d_cols],
+                    rhs=h_codes[g][:, moving].bitcast(FP8X4),
+                    rhs_scale=h_scales[g][:, moving],
+                    start=first_pass,
+                    stop=last_pass,
+                )
+            nc.tensor.matmul_mx(
+                out=acc_last[:],
+                lhsT=h_codes[g][:, last_block].bitcast(FP8X4),
+                lhsT_scale=h_scales[g][:, last_block],
+                rhs=w_codes[g][:].bitcast(FP8X4),
+                rhs_scale=w_scales[g][:],
+                start=first_pass,
+                stop=last_pass,
+            )
 
-        for s in range(ROUNDS + 2):
-            if 1 <= s <= ROUNDS:
-                quantise_h(s - 1)
-            if 2 <= s:
-                quantise_w(s - 2)
-            if s < ROUNDS:
-                transpose_u(s)
-                scale_u(s)
-                transpose_h(s)
-                quantise_us(s)
-                if s + LOADS_AHEAD < ROUNDS:
-                    load(s + LOADS_AHEAD)
-            if 1 <= s <= ROUNDS:
-                build_w(s - 1)
-            if 2 <= s:
-                apply_w(s - 2)
+        for turn in range(PASSES + 2):
+            if 1 <= turn <= PASSES:
+                quantise_h(turn - 1)
+            if 2 <= turn:
+                quantise_w(turn - 2)
+            if 1 <= turn <= PASSES:
+                quantise_us(turn - 1)
+            if turn < PASSES:
+                transpose_u(turn)
+                transpose_h(turn)
+                scale_u(turn)
+                next_load = turn // PASSES_PER_LOAD + LOADS_AHEAD
+                if turn % PASSES_PER_LOAD == PASSES_PER_LOAD - 1 and next_load < LOADS:
+                    load(next_load)
+            if 2 <= turn:
+                apply_w(turn - 2)
+            if 1 <= turn <= PASSES:
+                build_w(turn - 1)
 
         result = consts.tile([P, TOKEN_BLOCKS, D], F32)
-        for b in range(TOKEN_BLOCKS):
-            nc.vector.tensor_tensor(out=result[:, b, :], in0=acc[b][:], in1=bias_all[:], op=add)
-            nc.sync.dma_start(out=out_view[b], in_=result[:, b, :])
+        nc.vector.tensor_tensor(
+            out=result[:, MOVING_BLOCKS, :], in0=acc_last[:], in1=bias_all[:], op=add
+        )
+        nc.sync.dma_start(out=out_view[:, MOVING_BLOCKS, :], in_=result[:, MOVING_BLOCKS, :])
+        out_t = [consts.tile([P, MOVING_TOKENS], F32, name="out_t%d" % x) for x in range(D_HALVES)]
+        nc.scalar.copy(out=out_t[0][:], in_=acc_t[0][:])
+        nc.vector.tensor_copy(out=out_t[1][:], in_=acc_t[1][:])
+        blocks_per_bank = BANK_F32 // D
+        for first_block in range(0, MOVING_BLOCKS, blocks_per_bank):
+            bank = ring.tile([P, blocks_per_bank, D], F32, tag="bank", name="out_bank")
+            for y in range(blocks_per_bank):
+                tok_cols = slice((first_block + y) * P, (first_block + y + 1) * P)
+                for x in range(D_HALVES):
+                    nc.tensor.transpose(
+                        bank[:, y, x * P : (x + 1) * P], out_t[x][:, tok_cols], ident[:]
+                    )
+            blocks = slice(first_block, first_block + blocks_per_bank)
+            nc.vector.tensor_tensor(
+                out=result[:, blocks, :],
+                in0=bank[:],
+                in1=bias_all[:].unsqueeze(1).to_broadcast([P, blocks_per_bank, D]),
+                op=add,
+            )
+            nc.sync.dma_start(out=out_view[:, blocks, :], in_=result[:, blocks, :])

@@ -240,10 +240,9 @@ def tile_hybridsuperlayer_pb_k_kernel(
         for turn in range(PASSES + 2):
             if 1 <= turn <= PASSES:
                 quantise_h(turn - 1)
+                quantise_us(turn - 1)
             if 2 <= turn:
                 quantise_w(turn - 2)
-            if 1 <= turn <= PASSES:
-                quantise_us(turn - 1)
             if turn < PASSES:
                 transpose_u(turn)
                 transpose_h(turn)
@@ -251,10 +250,10 @@ def tile_hybridsuperlayer_pb_k_kernel(
                 next_load = turn // PASSES_PER_LOAD + LOADS_AHEAD
                 if turn % PASSES_PER_LOAD == PASSES_PER_LOAD - 1 and next_load < LOADS:
                     load(next_load)
-            if 2 <= turn:
-                apply_w(turn - 2)
             if 1 <= turn <= PASSES:
                 build_w(turn - 1)
+            if 2 <= turn:
+                apply_w(turn - 2)
 
         result = consts.tile([P, TOKEN_BLOCKS, D], F32)
         nc.vector.tensor_tensor(

@@ -29,7 +29,6 @@ ACC_BANKS = D_HALVES + 1
 RING_BANKS = 8 - ACC_BANKS
 
 PASSES_PER_LOAD = 2
-LOADS = PASSES // PASSES_PER_LOAD
 LOADS_AHEAD = 6
 LOAD_K = PASSES_PER_LOAD * K_PASS
 
@@ -43,9 +42,15 @@ def tile_hybridsuperlayer_pb_k_kernel(
     mult = mybir.AluOpType.mult
     add = mybir.AluOpType.add
 
-    h_view = h_gelu.flatten_outer_dims().rearrange("(b p) (i k) -> i p b k", p=P, k=LOAD_K)
-    u_view = c_proj_U.rearrange("(i x p e) r -> i p x (e r)", x=2 * PASSES_PER_LOAD, p=P, e=2)
+    h_flat = h_gelu.flatten_outer_dims()
     out_view = out.flatten_outer_dims().rearrange("(b p) d -> p b d", p=P)
+
+    load_first = list(range(PASSES_PER_LOAD)) + list(range(PASSES_PER_LOAD, PASSES, PASSES_PER_LOAD))
+    load_end = load_first[1:] + [PASSES]
+    home = {}
+    for i in range(len(load_first)):
+        for g in range(load_first[i], load_end[i]):
+            home[g] = (i, g - load_first[i])
 
     with ExitStack() as ctx:
         consts = ctx.enter_context(tc.tile_pool(name="consts", bufs=1))
@@ -59,10 +64,18 @@ def tile_hybridsuperlayer_pb_k_kernel(
         h_rows = {}
 
         def load(i):
-            u_rows[i] = loads.tile([P, 2 * PASSES_PER_LOAD, 2 * RANK], BF16, name="u_rows")
-            nc.sync.dma_start(out=u_rows[i][:], in_=u_view[i])
+            passes = load_end[i] - load_first[i]
+            k_range = slice(load_first[i] * K_PASS, load_end[i] * K_PASS)
             h_rows[i] = loads.tile([P, TOKEN_BLOCKS, LOAD_K], BF16, name="h_rows")
-            nc.sync.dma_start(out=h_rows[i][:], in_=h_view[i])
+            nc.sync.dma_start(
+                out=h_rows[i][:, :, 0 : passes * K_PASS],
+                in_=h_flat[:, k_range].rearrange("(b p) k -> p b k", p=P),
+            )
+            u_rows[i] = loads.tile([P, 2 * PASSES_PER_LOAD, 2 * RANK], BF16, name="u_rows")
+            nc.sync.dma_start(
+                out=u_rows[i][:, 0 : 2 * passes, :],
+                in_=c_proj_U[k_range, :].rearrange("(x p e) r -> p x (e r)", p=P, e=2),
+            )
 
         v_rows = consts.tile([P, D_HALVES, RANK], BF16)
         nc.scalar.dma_start(out=v_rows[:], in_=c_proj_V.rearrange("(x p) r -> p x r", p=P))
@@ -79,10 +92,9 @@ def tile_hybridsuperlayer_pb_k_kernel(
         ident = consts.tile([P, P], F32)
         make_identity(nc, ident[:])
 
-        s_pass = consts.tile([P, K_PASS, PACK], BF16)
+        s_bank = consts.tile([P, BANK_COLS, 2, 2], BF16)
         nc.vector.tensor_copy(
-            out=s_pass[:],
-            in_=s_word[:].rearrange("p half e -> p (half e)").unsqueeze(1).to_broadcast([P, K_PASS, PACK]),
+            out=s_bank[:], in_=s_word[:].unsqueeze(1).to_broadcast([P, BANK_COLS, 2, 2])
         )
 
         v_words = v_rows[:].bitcast(F32)
@@ -107,7 +119,6 @@ def tile_hybridsuperlayer_pb_k_kernel(
         acc_t = [acc_pool.tile([P, MOVING_TOKENS], F32, name="acc_t%d" % x) for x in range(D_HALVES)]
         acc_last = acc_pool.tile([P, D], F32)
 
-        u_t = {}
         us_t = {}
         us_codes = {}
         us_scales = {}
@@ -118,11 +129,10 @@ def tile_hybridsuperlayer_pb_k_kernel(
         w_codes = {}
         w_scales = {}
 
-        def transpose_u(g):
-            i, g_in_load = divmod(g, PASSES_PER_LOAD)
+        def transpose_scale_u(g):
+            i, place = home[g]
             u_words = u_rows[i][:].bitcast(F32)
-            u_t[g] = work.tile([P, K_PASS, PACK], BF16, name="u_t", align_bytes=64)
-            u_t_words = u_t[g][:].bitcast(F32)
+            us_t[g] = work.tile([P, K_PASS, PACK], BF16, name="us_t", align_bytes=64)
             for k_half in range(2):
                 bank = ring.tile([P, 2, BANK_COLS], F32, tag="bank", name="u_bank")
                 for e in range(2):
@@ -130,17 +140,16 @@ def tile_hybridsuperlayer_pb_k_kernel(
                         first = e * (RANK // 2) + half * P
                         nc.tensor.transpose(
                             bank[:, half, e * P : (e + 1) * P],
-                            u_words[:, 2 * g_in_load + k_half, first : first + P],
+                            u_words[:, 2 * place + k_half, first : first + P],
                             ident[:],
                         )
-                nc.scalar.copy(
-                    out=u_t_words[:, k_half * BANK_COLS : (k_half + 1) * BANK_COLS, :],
-                    in_=bank[:].rearrange("p half c -> p c half"),
+                cols = slice(k_half * BANK_COLS, (k_half + 1) * BANK_COLS)
+                nc.vector.tensor_tensor(
+                    out=us_t[g][:, cols, :].rearrange("p c (half e) -> p c half e", e=2),
+                    in0=bank[:].bitcast(BF16).rearrange("p half (c e) -> p c half e", e=2),
+                    in1=s_bank[:],
+                    op=mult,
                 )
-
-        def scale_u(g):
-            us_t[g] = work.tile([P, K_PASS, PACK], BF16, name="us_t", align_bytes=64)
-            nc.vector.tensor_tensor(out=us_t[g][:], in0=u_t[g][:], in1=s_pass[:], op=mult)
 
         def quantise_us(g):
             us_codes[g] = work.tile([P, K_PASS], U32, name="us_codes", align_bytes=64)
@@ -152,7 +161,7 @@ def tile_hybridsuperlayer_pb_k_kernel(
             )
 
         def transpose_h(g):
-            i, g_in_load = divmod(g, PASSES_PER_LOAD)
+            i, place = home[g]
             h_words = h_rows[i][:].bitcast(F32)
             h_t[g] = work.tile([P, TOKENS, PACK], BF16, name="h_t", align_bytes=64)
             h_t_words = h_t[g][:].bitcast(F32)
@@ -161,22 +170,20 @@ def tile_hybridsuperlayer_pb_k_kernel(
                 bank = ring.tile([P, 2, BANK_COLS], F32, tag="bank", name="h_bank")
                 for y in range(cols // P):
                     for half in range(2):
-                        first = (2 * g_in_load + half) * P
+                        first = (2 * place + half) * P
                         nc.tensor.transpose(
                             bank[:, half, y * P : (y + 1) * P],
                             h_words[:, first_col // P + y, first : first + P],
                             ident[:],
                         )
-                dest = h_t_words[:, first_col : first_col + cols, :]
-                filled = bank[:, :, 0:cols].rearrange("p half c -> p c half")
-                if cols == BANK_COLS:
-                    nc.scalar.copy(out=dest, in_=filled)
-                else:
-                    nc.vector.tensor_copy(out=dest, in_=filled)
+                nc.scalar.copy(
+                    out=h_t_words[:, first_col : first_col + cols, :],
+                    in_=bank[:, :, 0:cols].rearrange("p half c -> p c half"),
+                )
 
         def quantise_h(g):
-            h_codes[g] = work.tile([P, TOKENS], U32, name="h_codes", align_bytes=64)
-            h_scales[g] = work.tile([P, TOKENS], U8, name="h_scales", align_bytes=64)
+            h_codes[g] = work.tile([P, TOKENS], U32, name="h_codes", bufs=4, align_bytes=64)
+            h_scales[g] = work.tile([P, TOKENS], U8, name="h_scales", bufs=4, align_bytes=64)
             for cols in (slice(0, MOVING_TOKENS), slice(MOVING_TOKENS, TOKENS)):
                 nc.vector.quantize_mx(
                     out=h_codes[g][:, cols].bitcast(FP8X4),
@@ -237,32 +244,31 @@ def tile_hybridsuperlayer_pb_k_kernel(
                 stop=last_pass,
             )
 
-        for turn in range(PASSES + 2):
+        for turn in range(PASSES + 3):
+            if 3 <= turn:
+                quantise_w(turn - 3)
             if 1 <= turn <= PASSES:
                 quantise_h(turn - 1)
                 quantise_us(turn - 1)
-            if 2 <= turn:
-                quantise_w(turn - 2)
             if turn < PASSES:
-                transpose_u(turn)
                 transpose_h(turn)
-                scale_u(turn)
-                next_load = turn // PASSES_PER_LOAD + LOADS_AHEAD
-                if turn % PASSES_PER_LOAD == PASSES_PER_LOAD - 1 and next_load < LOADS:
-                    load(next_load)
-            if 1 <= turn <= PASSES:
-                build_w(turn - 1)
-            if 2 <= turn:
-                apply_w(turn - 2)
+                transpose_scale_u(turn)
+                i = home[turn][0]
+                if turn == load_end[i] - 1 and i + LOADS_AHEAD < len(load_first):
+                    load(i + LOADS_AHEAD)
+            if 2 <= turn <= PASSES + 1:
+                build_w(turn - 2)
+            if 3 <= turn:
+                apply_w(turn - 3)
 
         result = consts.tile([P, TOKEN_BLOCKS, D], F32)
+        out_t = [consts.tile([P, MOVING_TOKENS], F32, name="out_t%d" % x) for x in range(D_HALVES)]
+        nc.scalar.copy(out=out_t[0][:], in_=acc_t[0][:])
+        nc.vector.tensor_copy(out=out_t[1][:], in_=acc_t[1][:])
         nc.vector.tensor_tensor(
             out=result[:, MOVING_BLOCKS, :], in0=acc_last[:], in1=bias_all[:], op=add
         )
         nc.sync.dma_start(out=out_view[:, MOVING_BLOCKS, :], in_=result[:, MOVING_BLOCKS, :])
-        out_t = [consts.tile([P, MOVING_TOKENS], F32, name="out_t%d" % x) for x in range(D_HALVES)]
-        nc.scalar.copy(out=out_t[0][:], in_=acc_t[0][:])
-        nc.vector.tensor_copy(out=out_t[1][:], in_=acc_t[1][:])
         blocks_per_bank = BANK_F32 // D
         for first_block in range(0, MOVING_BLOCKS, blocks_per_bank):
             bank = ring.tile([P, blocks_per_bank, D], F32, tag="bank", name="out_bank")

from contextlib import ExitStack

import concourse.mybir as mybir
from concourse.masks import make_identity

BF16 = mybir.dt.bfloat16
F32 = mybir.dt.float32
U32 = mybir.dt.uint32
U8 = mybir.dt.uint8
FP8X4 = mybir.dt.float8_e4m3fn_x4

P = 128
PACK = 4
K_PASS = P * PACK

TOKENS = 640
TOKEN_BLOCKS = TOKENS // P
DFF = 16384
RANK = 512
D = 256
D_HALVES = D // P
PASSES = DFF // K_PASS

BANK_F32 = 512
BANK_COLS = BANK_F32 // 2
MOVING_TOKENS = BANK_F32
MOVING_BLOCKS = MOVING_TOKENS // P
ACC_BANKS = D_HALVES + 1
RING_BANKS = 8 - ACC_BANKS

PASSES_PER_LOAD = 2
LOADS_AHEAD = 6
LOAD_K = PASSES_PER_LOAD * K_PASS

FLOPS = 2 * DFF * RANK * D + 2 * TOKENS * DFF * D


def tile_hybridsuperlayer_pb_k_kernel(
    tc, h_gelu, c_proj_U, c_proj_S, c_proj_V, c_proj_bias, out
):
    nc = tc.nc
    mult = mybir.AluOpType.mult
    add = mybir.AluOpType.add

    h_flat = h_gelu.flatten_outer_dims()
    out_view = out.flatten_outer_dims().rearrange("(b p) d -> p b d", p=P)

    load_first = list(range(PASSES_PER_LOAD)) + list(range(PASSES_PER_LOAD, PASSES, PASSES_PER_LOAD))
    load_end = load_first[1:] + [PASSES]
    home = {}
    for i in range(len(load_first)):
        for g in range(load_first[i], load_end[i]):
            home[g] = (i, g - load_first[i])

    with ExitStack() as ctx:
        consts = ctx.enter_context(tc.tile_pool(name="consts", bufs=1))
        loads = ctx.enter_context(tc.tile_pool(name="loads", bufs=LOADS_AHEAD))
        work = ctx.enter_context(tc.tile_pool(name="work", bufs=3))
        acc_pool = ctx.enter_context(tc.psum_pool(name="acc", bufs=1))
        ring = ctx.enter_context(tc.psum_pool(name="ring", bufs=RING_BANKS))
        ctx.enter_context(tc.manual_schedule())

        u_rows = {}
        h_rows = {}

        def load(i):
            passes = load_end[i] - load_first[i]
            k_range = slice(load_first[i] * K_PASS, load_end[i] * K_PASS)
            h_rows[i] = loads.tile([P, TOKEN_BLOCKS, LOAD_K], BF16, name="h_rows")
            nc.sync.dma_start(
                out=h_rows[i][:, :, 0 : passes * K_PASS],
                in_=h_flat[:, k_range].rearrange("(b p) k -> p b k", p=P),
            )
            u_rows[i] = loads.tile([P, 2 * PASSES_PER_LOAD, 2 * RANK], BF16, name="u_rows")
            nc.sync.dma_start(
                out=u_rows[i][:, 0 : 2 * passes, :],
                in_=c_proj_U[k_range, :].rearrange("(x p e) r -> p x (e r)", p=P, e=2),
            )

        v_rows = consts.tile([P, D_HALVES, RANK], BF16)
        nc.scalar.dma_start(out=v_rows[:], in_=c_proj_V.rearrange("(x p) r -> p x r", p=P))
        s_word = consts.tile([P, 2, 2], BF16)
        with nc.allow_non_contiguous_dma(reason="512 values, two pairs to a partition, once"):
            nc.scalar.dma_start(
                out=s_word[:], in_=c_proj_S.rearrange("(half p e) -> p half e", half=2, p=P, e=2)
            )
        bias_all = consts.tile([P, D], BF16)
        nc.scalar.dma_start(out=bias_all[:], in_=c_proj_bias.partition_broadcast(P))
        for i in range(LOADS_AHEAD):
            load(i)

        ident = consts.tile([P, P], F32)
        make_identity(nc, ident[:])

        s_bank = consts.tile([P, BANK_COLS, 2, 2], BF16)
        nc.vector.tensor_copy(
            out=s_bank[:], in_=s_word[:].unsqueeze(1).to_broadcast([P, BANK_COLS, 2, 2])
        )

        v_words = v_rows[:].bitcast(F32)
        v_bank = ring.tile([P, 2, BANK_COLS], F32, tag="bank")
        for x in range(D_HALVES):
            for half in range(2):
                nc.tensor.transpose(
                    v_bank[:, half, x * P : (x + 1) * P],
                    v_words[:, x, half * P : (half + 1) * P],
                    ident[:],
                )
        v_t = consts.tile([P, D, PACK], BF16, align_bytes=64)
        nc.scalar.copy(out=v_t[:].bitcast(F32), in_=v_bank[:].rearrange("p half c -> p c half"))
        v_codes = consts.tile([P, D], U32, align_bytes=64)
        v_scales = consts.tile([P, D], U8, align_bytes=64)
        nc.vector.quantize_mx(
            out=v_codes[:].bitcast(FP8X4),
            scales=v_scales[:],
            in_=v_t[:].rearrange("p c t -> p (c t)"),
        )

        acc_t = [acc_pool.tile([P, MOVING_TOKENS], F32, name="acc_t%d" % x) for x in range(D_HALVES)]
        acc_last = acc_pool.tile([P, D], F32)

        us_t = {}
        us_codes = {}
        us_scales = {}
        h_t = {}
        h_codes = {}
        h_scales = {}
        w_t = {}
        w_codes = {}
        w_scales = {}

        def transpose_scale_u(g):
            i, place = home[g]
            u_words = u_rows[i][:].bitcast(F32)
            us_t[g] = work.tile([P, K_PASS, PACK], BF16, name="us_t", align_bytes=64)
            for k_half in range(2):
                bank = ring.tile([P, 2, BANK_COLS], F32, tag="bank", name="u_bank")
                for e in range(2):
                    for half in range(2):
                        first = e * (RANK // 2) + half * P
                        nc.tensor.transpose(
                            bank[:, half, e * P : (e + 1) * P],
                            u_words[:, 2 * place + k_half, first : first + P],
                            ident[:],
                        )
                cols = slice(k_half * BANK_COLS, (k_half + 1) * BANK_COLS)
                nc.vector.tensor_tensor(
                    out=us_t[g][:, cols, :].rearrange("p c (half e) -> p c half e", e=2),
                    in0=bank[:].bitcast(BF16).rearrange("p half (c e) -> p c half e", e=2),
                    in1=s_bank[:],
                    op=mult,
                )

        def quantise_us(g):
            us_codes[g] = work.tile([P, K_PASS], U32, name="us_codes", align_bytes=64)
            us_scales[g] = work.tile([P, K_PASS], U8, name="us_scales", align_bytes=64)
            nc.vector.quantize_mx(
                out=us_codes[g][:].bitcast(FP8X4),
                scales=us_scales[g][:],
                in_=us_t[g][:].rearrange("p c t -> p (c t)"),
            )

        def transpose_h(g):
            i, place = home[g]
            h_words = h_rows[i][:].bitcast(F32)
            h_t[g] = work.tile([P, TOKENS, PACK], BF16, name="h_t", align_bytes=64)
            h_t_words = h_t[g][:].bitcast(F32)
            for first_col in range(0, TOKENS, BANK_COLS):
                cols = min(BANK_COLS, TOKENS - first_col)
                bank = ring.tile([P, 2, BANK_COLS], F32, tag="bank", name="h_bank")
                for y in range(cols // P):
                    for half in range(2):
                        first = (2 * place + half) * P
                        nc.tensor.transpose(
                            bank[:, half, y * P : (y + 1) * P],
                            h_words[:, first_col // P + y, first : first + P],
                            ident[:],
                        )
                nc.scalar.copy(
                    out=h_t_words[:, first_col : first_col + cols, :],
                    in_=bank[:, :, 0:cols].rearrange("p half c -> p c half"),
                )

        def quantise_h(g):
            h_codes[g] = work.tile([P, TOKENS], U32, name="h_codes", bufs=4, align_bytes=64)
            h_scales[g] = work.tile([P, TOKENS], U8, name="h_scales", bufs=4, align_bytes=64)
            for cols in (slice(0, MOVING_TOKENS), slice(MOVING_TOKENS, TOKENS)):
                nc.vector.quantize_mx(
                    out=h_codes[g][:, cols].bitcast(FP8X4),
                    scales=h_scales[g][:, cols],
                    in_=h_t[g][:, cols, :].rearrange("p c t -> p (c t)"),
                )

        def build_w(g):
            w_t[g] = work.tile([P, D, PACK], BF16, name="w_t", align_bytes=64)
            for x in range(D_HALVES):
                d_cols = slice(x * P, (x + 1) * P)
                bank = ring.tile([P, PACK, P], F32, tag="bank", name="w_bank")
                for t in range(PACK):
                    k_cols = slice(t * P, (t + 1) * P)
                    nc.tensor.matmul_mx(
                        out=bank[:, t, :],
                        lhsT=us_codes[g][:, k_cols].bitcast(FP8X4),
                        lhsT_scale=us_scales[g][:, k_cols],
                        rhs=v_codes[:, d_cols].bitcast(FP8X4),
                        rhs_scale=v_scales[:, d_cols],
                        start=True,
                        stop=True,
                    )
                nc.scalar.copy(out=w_t[g][:, d_cols, :], in_=bank[:].rearrange("p t d -> p d t"))

        def quantise_w(g):
            w_codes[g] = work.tile([P, D], U32, name="w_codes", align_bytes=64)
            w_scales[g] = work.tile([P, D], U8, name="w_scales", align_bytes=64)
            nc.vector.quantize_mx(
                out=w_codes[g][:].bitcast(FP8X4),
                scales=w_scales[g][:],
                in_=w_t[g][:].rearrange("p d t -> p (d t)"),
            )

        def apply_w(g):
            first_pass = g == 0
            last_pass = g == PASSES - 1
            moving = slice(0, MOVING_TOKENS)
            last_block = slice(MOVING_TOKENS, TOKENS)
            for x in range(D_HALVES):
                d_cols = slice(x * P, (x + 1) * P)
                nc.tensor.matmul_mx(
                    out=acc_t[x][:],
                    lhsT=w_codes[g][:, d_cols].bitcast(FP8X4),
                    lhsT_scale=w_scales[g][:, d_cols],
                    rhs=h_codes[g][:, moving].bitcast(FP8X4),
                    rhs_scale=h_scales[g][:, moving],
                    start=first_pass,
                    stop=last_pass,
                )
            nc.tensor.matmul_mx(
                out=acc_last[:],
                lhsT=h_codes[g][:, last_block].bitcast(FP8X4),
                lhsT_scale=h_scales[g][:, last_block],
                rhs=w_codes[g][:].bitcast(FP8X4),
                rhs_scale=w_scales[g][:],
                start=first_pass,
                stop=last_pass,
            )

        for turn in range(PASSES + 3):
            if 3 <= turn:
                quantise_w(turn - 3)
            if 1 <= turn <= PASSES:
                quantise_h(turn - 1)
                quantise_us(turn - 1)
            if turn < PASSES:
                transpose_h(turn)
                transpose_scale_u(turn)
                i = home[turn][0]
                if turn == load_end[i] - 1 and i + LOADS_AHEAD < len(load_first):
                    load(i + LOADS_AHEAD)
            if 2 <= turn <= PASSES + 1:
                build_w(turn - 2)
            if 3 <= turn:
                apply_w(turn - 3)

        result = consts.tile([P, TOKEN_BLOCKS, D], F32)
        out_t = [consts.tile([P, MOVING_TOKENS], F32, name="out_t%d" % x) for x in range(D_HALVES)]
        nc.scalar.copy(out=out_t[0][:], in_=acc_t[0][:])
        nc.vector.tensor_copy(out=out_t[1][:], in_=acc_t[1][:])
        nc.vector.tensor_tensor(
            out=result[:, MOVING_BLOCKS, :], in0=acc_last[:], in1=bias_all[:], op=add
        )
        nc.sync.dma_start(out=out_view[:, MOVING_BLOCKS, :], in_=result[:, MOVING_BLOCKS, :])
        blocks_per_bank = BANK_F32 // D
        for first_block in range(0, MOVING_BLOCKS, blocks_per_bank):
            bank = ring.tile([P, blocks_per_bank, D], F32, tag="bank", name="out_bank")
            for y in range(blocks_per_bank):
                tok_cols = slice((first_block + y) * P, (first_block + y + 1) * P)
                for x in range(D_HALVES):
                    nc.tensor.transpose(
                        bank[:, y, x * P : (x + 1) * P], out_t[x][:, tok_cols], ident[:]
                    )
            blocks = slice(first_block, first_block + blocks_per_bank)
            nc.vector.tensor_tensor(
                out=result[:, blocks, :],
                in0=bank[:],
                in1=bias_all[:].unsqueeze(1).to_broadcast([P, blocks_per_bank, D]),
                op=add,
            )
            nc.sync.dma_start(out=out_view[:, blocks, :], in_=result[:, blocks, :])
